import numpy as np
import ml_dtypes


def mxq(x, axis, fmt="e4m3"):
    dtype, down = {"e4m3": (ml_dtypes.float8_e4m3fn, 7), "e5m2": (ml_dtypes.float8_e5m2, 14)}[fmt]
    v = np.moveaxis(np.asarray(x, np.float32).astype(ml_dtypes.bfloat16).astype(np.float64), axis, -1)
    blocks = v.reshape(v.shape[:-1] + (-1, 32))
    amax = np.abs(blocks).max(-1, keepdims=True)
    byte = np.maximum(np.where(amax > 0, np.frexp(amax)[1] - 1 + 127, 0) - down, 1)
    scale = np.exp2(byte - 127.0)
    codes = (blocks / scale).astype(np.float32).astype(dtype).astype(np.float64)
    return np.moveaxis((codes * scale).reshape(v.shape), -1, axis)


WIDE = False


def mx_kscale(k):
    if not WIDE:
        return np.ones(k)
    levels = np.array([10, -10, 5, -5, 0])
    if k % 512:
        return np.exp2(np.random.permutation(np.resize(levels, k // 32))).repeat(32)
    a = np.empty((k // 512, 16))
    for p in range(k // 512):
        a[p, :8] = np.random.permutation(np.resize(levels, 8))
        for g in range(8):
            far = levels[np.abs(levels - a[p, g]) >= 10]
            a[p, g + 8] = far[np.random.randint(len(far))]
    return np.exp2(a.ravel()).repeat(32)


BF16 = ml_dtypes.bfloat16


def bf(x):
    return np.asarray(x, np.float32).astype(BF16)


def f64(x):
    return np.asarray(x).astype(np.float64)


B, D, E = 32, 1024, 256
S = E // 2


def rope(y):
    n = y.shape[-1]
    inv_freq = 1.0 / (10000.0 ** (np.arange(0.0, n, 2.0) / n))
    freqs = inv_freq * np.arange(y.shape[1], dtype=np.float64)
    sin = np.sin(freqs)[None, :, None]
    cos = np.cos(freqs)[None, :, None]
    y1 = y[..., ::2]
    y2 = y[..., 1::2]
    return np.concatenate([y1 * cos - y2 * sin, y1 * sin + y2 * cos], axis=-1)


def setup_inputs():
    s = mx_kscale(D)
    return {"x": bf(np.random.standard_normal((B, S, D)) * s),
            "Wk": bf(np.random.standard_normal((E, D)) / np.sqrt(D) / s[None, :]),
            "bk": bf(np.random.standard_normal(E) * 0.3),
            "Wq": bf(np.random.standard_normal((E, D)) / np.sqrt(D) / s[None, :]),
            "bq": bf(np.random.standard_normal(E) * 0.3),
            "Wv": bf(np.random.standard_normal((E, D)) / np.sqrt(D) / s[None, :]),
            "bv": bf(np.random.standard_normal(E) * 0.3)}


def reference(x, Wk, bk, Wq, bq, Wv, bv):
    xq = mxq(f64(x), 2, "e4m3")
    K = rope((xq @ mxq(f64(Wk), 1, "e4m3").T) + f64(bk))
    Q = rope((xq @ mxq(f64(Wq), 1, "e4m3").T) + f64(bq))
    V = (xq @ mxq(f64(Wv), 1, "e4m3").T) + f64(bv)
    return (K, Q, V)

@@ -1,0 +1,281 @@
+import math
+from contextlib import ExitStack
+
+import concourse.mybir as mybir
+from concourse.masks import make_identity
+
+FLOPS = 2 * 4096 * 1024 * 768
+
+F32 = mybir.dt.float32
+BF16 = mybir.dt.bfloat16
+I32 = mybir.dt.int32
+U32 = mybir.dt.uint32
+U8 = mybir.dt.uint8
+FP8X4 = mybir.dt.float8_e4m3fn_x4
+ALU = mybir.AluOpType
+ACT = mybir.ActivationFunctionType
+
+P = 128
+D = 1024
+E = 256
+TOKENS = 4096
+PAIRS = TOKENS // (2 * P)
+
+
+def tile_attention_t_kernel(tc, x, Wk, bk, Wq, bq, Wv, bv, out_0, out_1, out_2):
+    nc = tc.nc
+    with ExitStack() as ctx:
+        ctx.enter_context(tc.manual_schedule())
+        const = ctx.enter_context(tc.tile_pool(name="const", bufs=1))
+        xpool = ctx.enter_context(tc.tile_pool(name="xpool", bufs=1))
+        gpool = ctx.enter_context(tc.tile_pool(name="gpool", bufs=2))
+        cpool = ctx.enter_context(tc.tile_pool(name="cpool", bufs=4))
+        tpool = ctx.enter_context(tc.tile_pool(name="tpool", bufs=4))
+        opool = ctx.enter_context(tc.tile_pool(name="opool", bufs=8))
+        ps_t = ctx.enter_context(tc.psum_pool(name="ps_t", bufs=2))
+        ps_kq = ctx.enter_context(tc.psum_pool(name="ps_kq", bufs=4))
+        ps_v = ctx.enter_context(tc.psum_pool(name="ps_v", bufs=2))
+
+        xv = x.flatten_outer_dims().rearrange("(i q s) d -> i q (s d)", q=P, s=2)
+        outs = [
+            o.flatten_outer_dims().rearrange("(i q s) e -> i q (s e)", q=P, s=2)
+            for o in (out_0, out_1, out_2)
+        ]
+
+        bland = const.tile([P, 3 * E], BF16, name="bland")
+        for n, b in enumerate((bk, bq, bv)):
+            nc.sync.dma_start(out=bland[0:1, n * E:(n + 1) * E], in_=b.rearrange("(o e) -> o e", o=1))
+        wraw = []
+        for n in range(3):
+            wraw.append(const.tile([P, 2 * D], BF16, name="wraw%d" % n))
+        xs = []
+        for i in range(PAIRS):
+            xs.append(xpool.tile([P, 2 * D], BF16, name="xs%d" % i))
+        nc.sync.dma_start(out=wraw[0][:], in_=Wk.rearrange("(j h) d -> j (h d)", h=2))
+        nc.sync.dma_start(out=wraw[1][:], in_=Wq.rearrange("(j h) d -> j (h d)", h=2))
+        nc.sync.dma_start(out=xs[0][:], in_=xv[0])
+        nc.sync.dma_start(
+            out=wraw[2][:].rearrange("j (h d) -> j h d", h=2),
+            in_=Wv.rearrange("(h j) d -> j h d", h=2),
+        )
+        for i in range(1, PAIRS):
+            nc.sync.dma_start(out=xs[i][:], in_=xv[i])
+
+        brow = const.tile([P, 3 * E], BF16, name="brow")
+        ones = const.tile([P, P], BF16, name="ones")
+        nc.vector.memset(brow[:], 0.0)
+        nc.vector.memset(ones[:], 1.0)
+        pos_i = const.tile([P, 2], I32, name="pos_i")
+        nc.gpsimd.iota(pos_i[:], pattern=[[1, 2]], base=0, channel_multiplier=2)
+        ident = const.tile([P, P], F32, name="ident")
+        make_identity(nc, ident[:])
+
+        pos_m = const.tile([P, 2], I32, name="pos_m")
+        nc.vector.tensor_single_scalar(out=pos_m[:], in_=pos_i[:], scalar=127, op=ALU.bitwise_and)
+        pos_f = const.tile([P, 2], F32, name="pos_f")
+        nc.vector.tensor_copy(out=pos_f[:], in_=pos_m[:])
+        decay = const.tile([P, 2], F32, name="decay")
+        nc.scalar.activation(out=decay[:], in_=pos_f[:], func=ACT.Exp, scale=-math.log(10000.0) / 128.0)
+        theta = const.tile([P, 2], F32, name="theta")
+        nc.vector.tensor_tensor(out=theta[:], in0=pos_f[:], in1=decay[:], op=ALU.mult)
+        s_half = const.tile([P, 2], F32, name="s_half")
+        s_quart = const.tile([P, 2], F32, name="s_quart")
+        nc.scalar.activation(out=s_half[:], in_=theta[:], func=ACT.Sin, scale=0.5)
+        nc.scalar.activation(out=s_quart[:], in_=theta[:], func=ACT.Sin, scale=0.25)
+
+        nc.vector.tensor_copy(out=brow[0:1, :], in_=bland[0:1, :])
+        bkq_ps = ps_kq.tile([P, 2 * E], F32, name="bkq_ps", tag="kq")
+        bv_ps = ps_v.tile([P, 2, E], F32, name="bv_ps", tag="v")
+        nc.tensor.matmul(out=bkq_ps[:], lhsT=ones[:], rhs=brow[:, 0:2 * E], start=True, stop=True)
+        nc.tensor.matmul(out=bv_ps[:, 0, :], lhsT=ones[:], rhs=brow[:, 2 * E:3 * E], start=True, stop=True)
+        b_eo = const.tile([P, 2 * E], F32, name="b_eo")
+        b_sw = const.tile([P, 2 * E], F32, name="b_sw")
+        b_v = const.tile([P, E], F32, name="b_v")
+        bkq_view = bkq_ps[:].rearrange("p (w j h) -> p h w j", w=2, h=2)
+        nc.scalar.copy(out=b_eo[:].rearrange("p (h w j) -> p h w j", h=2, w=2), in_=bkq_view)
+        nc.vector.tensor_copy(out=b_sw[:, 0:E].rearrange("p (w j) -> p w j", w=2), in_=bkq_view[:, 1])
+        nc.vector.tensor_scalar(
+            out=b_sw[:, E:2 * E].rearrange("p (w j) -> p w j", w=2), in0=bkq_view[:, 0],
+            scalar1=-1.0, scalar2=None, op0=ALU.mult,
+        )
+        nc.scalar.copy(out=b_v[:], in_=bv_ps[:, 0, :])
+
+        sq_q = const.tile([P, 2], F32, name="sq_q")
+        c_half = const.tile([P, 2], F32, name="c_half")
+        sin_t = const.tile([P, 2], F32, name="sin_t")
+        sq_h = const.tile([P, 2], F32, name="sq_h")
+        cos_t = const.tile([P, 2], F32, name="cos_t")
+        nc.vector.tensor_tensor(out=sq_q[:], in0=s_quart[:], in1=s_quart[:], op=ALU.mult)
+        nc.vector.tensor_tensor(out=sq_h[:], in0=s_half[:], in1=s_half[:], op=ALU.mult)
+        nc.vector.tensor_scalar(out=c_half[:], in0=sq_q[:], scalar1=-2.0, scalar2=1.0, op0=ALU.mult, op1=ALU.add)
+        nc.vector.tensor_scalar(out=cos_t[:], in0=sq_h[:], scalar1=-2.0, scalar2=1.0, op0=ALU.mult, op1=ALU.add)
+        nc.vector.scalar_tensor_tensor(
+            out=sin_t[:], in0=s_half[:], scalar=2.0, in1=c_half[:], op0=ALU.mult, op1=ALU.mult
+        )
+
+        wgrp = const.tile([P, 2 * 6 * 4 * P], BF16, name="wgrp", align_bytes=64)
+        wcod = const.tile([P, 2, 6 * P], U32, name="wcod", align_bytes=64)
+        wscl = const.tile([P, 2, 6 * P], U8, name="wscl", align_bytes=64)
+        wgrp_w = wgrp[:].bitcast(F32).rearrange("p (g c r u) -> p g c r u", g=2, c=6, u=2)
+
+        def transposes(words, pool, tag):
+            tb = pool.tile([P, 4, P], F32, name="tb_" + tag, tag=tag)
+            for c in range(4):
+                g, u = divmod(c, 2)
+                nc.tensor.transpose(tb[:, c, :], words[:, 2 * P * g + u:2 * P * (g + 1):2], ident[:])
+            return tb[:].rearrange("p (g u) q -> p g q u", u=2)
+
+        def weight_tile(col, raw, half, on_vector):
+            pool, tag = (ps_kq, "kq") if col < 4 else (ps_v, "v")
+            src = transposes(raw[:].bitcast(F32)[:, half * (D // 2):(half + 1) * (D // 2)], pool, tag)
+            if on_vector:
+                nc.vector.tensor_copy(out=wgrp_w[:, :, col], in_=src)
+            else:
+                nc.scalar.copy(out=wgrp_w[:, :, col], in_=src)
+
+        def weight_quant(lo, hi):
+            for g in range(2):
+                nc.vector.quantize_mx(
+                    out=wcod[:, g, lo * P:hi * P].bitcast(FP8X4),
+                    scales=wscl[:, g, lo * P:hi * P],
+                    in_=wgrp[:, (g * 6 + lo) * 4 * P:(g * 6 + hi) * 4 * P],
+                )
+
+        grouped = {}
+        codes = {}
+        banks = {}
+        parts = {}
+        cosines = {}
+
+        def front_a(i):
+            grp = gpool.tile([P, 2 * D], BF16, name="grp", tag="grp", align_bytes=64)
+            grp_w = grp[:].bitcast(F32).rearrange("p (s g q u) -> p s g q u", s=2, g=2, u=2)
+            words = xs[i][:].bitcast(F32)
+            for s in range(2):
+                src = transposes(words[:, s * (D // 2):(s + 1) * (D // 2)], ps_t, "t")
+                nc.scalar.copy(out=grp_w[:, s], in_=src)
+            grouped[i] = grp
+
+        def front_b(i):
+            cod = cpool.tile([P, 4 * P], U32, name="cod", tag="cod", align_bytes=64)
+            scl = cpool.tile([P, 4 * P], U8, name="scl", tag="scl", align_bytes=64)
+            nc.vector.quantize_mx(out=cod[:].bitcast(FP8X4), scales=scl[:], in_=grouped[i][:])
+            codes[i] = (cod, scl)
+
+        bias_x = const.tile([P, 2, 2 * E], F32, name="bias_x")
+
+        def bias_table(s):
+            tmp = tpool.tile([P, 2 * E], F32, name="tmp", tag="tmp", bufs=2)
+            nc.scalar.activation(out=tmp[:], in_=b_sw[:], func=ACT.Copy, scale=cos_t[:, s:s + 1])
+            nc.vector.scalar_tensor_tensor(
+                out=bias_x[:, s, :], in0=b_eo[:], scalar=sin_t[:, s:s + 1], in1=tmp[:],
+                op0=ALU.mult, op1=ALU.add,
+            )
+
+        def mx_pair(i):
+            cod, scl = codes[i]
+            kq = []
+            for s in range(2):
+                acc = ps_kq.tile([P, 2 * E], F32, name="kq", tag="kq")
+                for g in range(2):
+                    cols = slice((2 * s + g) * P, (2 * s + g + 1) * P)
+                    nc.tensor.matmul_mx(
+                        out=acc[:], lhsT=cod[:, cols].bitcast(FP8X4), lhsT_scale=scl[:, cols],
+                        rhs=wcod[:, g, 0:4 * P].bitcast(FP8X4), rhs_scale=wscl[:, g, 0:4 * P],
+                        start=(g == 0), stop=(g == 1),
+                    )
+                kq.append(acc)
+            vb = ps_v.tile([P, 2, E], F32, name="vb", tag="v")
+            for s in range(2):
+                for g in range(2):
+                    cols = slice((2 * s + g) * P, (2 * s + g + 1) * P)
+                    nc.tensor.matmul_mx(
+                        out=vb[:, s, :], lhsT=cod[:, cols].bitcast(FP8X4), lhsT_scale=scl[:, cols],
+                        rhs=wcod[:, g, 4 * P:6 * P].bitcast(FP8X4), rhs_scale=wscl[:, g, 4 * P:6 * P],
+                        start=(g == 0), stop=(g == 1),
+                    )
+            banks[i] = (kq, vb)
+
+        def halves(ap):
+            return ap.rearrange("p (w j) -> p w j", w=2)
+
+        def pool_adds_b1(i):
+            return 0 < i < PAIRS - 1
+
+        def times_cos(i):
+            kq = banks[i][0]
+            c_pair = tpool.tile([P, 2, 2 * E], F32, name="c_pair", tag="c_pair")
+            for s in range(2):
+                width = 2 * E if (s == 1 and pool_adds_b1(i)) else E
+                nc.scalar.activation(
+                    out=c_pair[:, s, 0:width], in_=kq[s][:, 0:width], func=ACT.Copy, scale=cos_t[:, s:s + 1]
+                )
+            cosines[i] = c_pair
+
+        def times_sin(i):
+            kq = banks[i][0]
+            t_pair = tpool.tile([P, 2, 2 * E], F32, name="t_pair", tag="t_pair")
+            for s in range(2):
+                nc.vector.scalar_tensor_tensor(
+                    out=t_pair[:, s, :], in0=kq[s][:], scalar=sin_t[:, s:s + 1], in1=bias_x[:, s, :],
+                    op0=ALU.mult, op1=ALU.add,
+                )
+            parts[i] = t_pair
+
+        def back_second(i):
+            kq, vb = banks[i]
+            t_pair = parts[i]
+            c_pair = cosines[i]
+            o = opool.tile([P, 3, 2, E], F32, name="stage", tag="stage")
+            nc.gpsimd.tensor_tensor(
+                out=o[:, 0:2, :, 0:P],
+                in0=c_pair[:, :, 0:E].rearrange("p s (w j) -> p w s j", w=2),
+                in1=t_pair[:, :, E:2 * E].rearrange("p s (w j) -> p w s j", w=2),
+                op=ALU.subtract,
+            )
+            for s in range(2):
+                if s == 1 and pool_adds_b1(i):
+                    nc.gpsimd.tensor_tensor(
+                        out=o[:, 0:2, s, P:2 * P], in0=halves(c_pair[:, s, E:2 * E]),
+                        in1=halves(t_pair[:, s, 0:E]), op=ALU.add,
+                    )
+                else:
+                    nc.vector.scalar_tensor_tensor(
+                        out=o[:, 0:2, s, P:2 * P], in0=halves(kq[s][:, E:2 * E]), scalar=cos_t[:, s:s + 1],
+                        in1=halves(t_pair[:, s, 0:E]), op0=ALU.mult, op1=ALU.add,
+                    )
+            nc.vector.tensor_tensor(
+                out=o[:, 2, :, :], in0=vb[:], in1=b_v[:].unsqueeze(1).to_broadcast([P, 2, E]), op=ALU.add
+            )
+            for n in (2, 0, 1):
+                nc.sync.dma_start(out=outs[n][i], in_=o[:, n, :, :].rearrange("p s e -> p (s e)"))
+
+        weight_tile(0, wraw[0], 0, False)
+        weight_tile(2, wraw[0], 1, True)
+        weight_tile(1, wraw[1], 0, False)
+        weight_tile(3, wraw[1], 1, True)
+        weight_quant(0, 4)
+        front_a(0)
+        front_b(0)
+        weight_tile(4, wraw[2], 0, False)
+        weight_tile(5, wraw[2], 1, False)
+        weight_quant(4, 6)
+        front_a(1)
+        front_b(1)
+        mx_pair(0)
+        bias_table(0)
+        bias_table(1)
+        times_cos(0)
+        front_a(2)
+        mx_pair(1)
+        for i in range(PAIRS):
+            if i + 1 < PAIRS:
+                times_cos(i + 1)
+            times_sin(i)
+            if i + 2 < PAIRS:
+                front_b(i + 2)
+            back_second(i)
+            if i + 3 < PAIRS:
+                front_a(i + 3)
+            if i + 2 < PAIRS:
+                mx_pair(i + 2)

@@ -44,14 +44,15 @@ def tile_attention_t_kernel(tc, x, Wk, bk, Wq, bq, Wv, bv, out_0, out_1, out_2):
 
         bland = const.tile([P, 3 * E], BF16, name="bland")
         for n, b in enumerate((bk, bq, bv)):
-            nc.sync.dma_start(out=bland[0:1, n * E:(n + 1) * E], in_=b.rearrange("(o e) -> o e", o=1))
+            nc.scalar.dma_start(out=bland[0:1, n * E:(n + 1) * E], in_=b.rearrange("(o e) -> o e", o=1))
         wraw = []
         for n in range(3):
             wraw.append(const.tile([P, 2 * D], BF16, name="wraw%d" % n))
         xs = []
         for i in range(PAIRS):
             xs.append(xpool.tile([P, 2 * D], BF16, name="xs%d" % i))
-        nc.sync.dma_start(out=wraw[0][:], in_=Wk.rearrange("(j h) d -> j (h d)", h=2))
+        for h in range(2):
+            nc.sync.dma_start(out=wraw[0][:, h * D:(h + 1) * D], in_=Wk.rearrange("(j h) d -> j (h d)", h=2)[:, h * D:(h + 1) * D])
         nc.sync.dma_start(out=wraw[1][:], in_=Wq.rearrange("(j h) d -> j (h d)", h=2))
         nc.sync.dma_start(out=xs[0][:], in_=xv[0])
         nc.sync.dma_start(
@@ -65,6 +66,8 @@ def tile_attention_t_kernel(tc, x, Wk, bk, Wq, bq, Wv, bv, out_0, out_1, out_2):
         ones = const.tile([P, P], BF16, name="ones")
         nc.vector.memset(brow[:], 0.0)
         nc.vector.memset(ones[:], 1.0)
+        zeros = const.tile([P, 2 * E], BF16, name="zeros")
+        nc.gpsimd.memset(zeros[:], 0.0)
         pos_i = const.tile([P, 2], I32, name="pos_i")
         nc.gpsimd.iota(pos_i[:], pattern=[[1, 2]], base=0, channel_multiplier=2)
         ident = const.tile([P, P], F32, name="ident")
@@ -82,6 +85,15 @@ def tile_attention_t_kernel(tc, x, Wk, bk, Wq, bq, Wv, bv, out_0, out_1, out_2):
         s_quart = const.tile([P, 2], F32, name="s_quart")
         nc.scalar.activation(out=s_half[:], in_=theta[:], func=ACT.Sin, scale=0.5)
         nc.scalar.activation(out=s_quart[:], in_=theta[:], func=ACT.Sin, scale=0.25)
+
+        for i in range(5):
+            warm_ps = ps_t.tile([P, 2 * E], F32, name="warm_ps", tag="t")
+            nc.tensor.matmul(out=warm_ps[:], lhsT=ones[:], rhs=zeros[:], start=True, stop=True)
+
+        def dummy(n):
+            for i in range(n):
+                warm_ps = ps_t.tile([P, 2 * E], F32, name="warm_ps", tag="t")
+                nc.tensor.matmul(out=warm_ps[:], lhsT=ones[:], rhs=zeros[:], start=True, stop=True)
 
         nc.vector.tensor_copy(out=brow[0:1, :], in_=bland[0:1, :])
         bkq_ps = ps_kq.tile([P, 2 * E], F32, name="bkq_ps", tag="kq")
@@ -252,13 +264,16 @@ def tile_attention_t_kernel(tc, x, Wk, bk, Wq, bq, Wv, bv, out_0, out_1, out_2):
 
         weight_tile(0, wraw[0], 0, False)
         weight_tile(2, wraw[0], 1, True)
+        dummy(2)
         weight_tile(1, wraw[1], 0, False)
         weight_tile(3, wraw[1], 1, True)
+        dummy(2)
         weight_quant(0, 4)
         front_a(0)
         front_b(0)
         weight_tile(4, wraw[2], 0, False)
         weight_tile(5, wraw[2], 1, False)
+        dummy(2)
         weight_quant(4, 6)
         front_a(1)
         front_b(1)

@@ -44,7 +44,7 @@ def tile_attention_t_kernel(tc, x, Wk, bk, Wq, bq, Wv, bv, out_0, out_1, out_2):
 
         bland = const.tile([P, 3 * E], BF16, name="bland")
         for n, b in enumerate((bk, bq, bv)):
-            nc.scalar.dma_start(out=bland[0:1, n * E:(n + 1) * E], in_=b.rearrange("(o e) -> o e", o=1))
+            nc.sync.dma_start(out=bland[0:1, n * E:(n + 1) * E], in_=b.rearrange("(o e) -> o e", o=1))
         wraw = []
         for n in range(3):
             wraw.append(const.tile([P, 2 * D], BF16, name="wraw%d" % n))
@@ -68,6 +68,12 @@ def tile_attention_t_kernel(tc, x, Wk, bk, Wq, bq, Wv, bv, out_0, out_1, out_2):
         nc.vector.memset(ones[:], 1.0)
         zeros = const.tile([P, 2 * E], BF16, name="zeros")
         nc.gpsimd.memset(zeros[:], 0.0)
+
+        def raise_clock(n):
+            for i in range(n):
+                idle = ps_t.tile([P, 2 * E], F32, name="idle", tag="t")
+                nc.tensor.matmul(out=idle[:], lhsT=ones[:], rhs=zeros[:], start=True, stop=True)
+
         pos_i = const.tile([P, 2], I32, name="pos_i")
         nc.gpsimd.iota(pos_i[:], pattern=[[1, 2]], base=0, channel_multiplier=2)
         ident = const.tile([P, P], F32, name="ident")
@@ -86,14 +92,7 @@ def tile_attention_t_kernel(tc, x, Wk, bk, Wq, bq, Wv, bv, out_0, out_1, out_2):
         nc.scalar.activation(out=s_half[:], in_=theta[:], func=ACT.Sin, scale=0.5)
         nc.scalar.activation(out=s_quart[:], in_=theta[:], func=ACT.Sin, scale=0.25)
 
-        for i in range(5):
-            warm_ps = ps_t.tile([P, 2 * E], F32, name="warm_ps", tag="t")
-            nc.tensor.matmul(out=warm_ps[:], lhsT=ones[:], rhs=zeros[:], start=True, stop=True)
-
-        def dummy(n):
-            for i in range(n):
-                warm_ps = ps_t.tile([P, 2 * E], F32, name="warm_ps", tag="t")
-                nc.tensor.matmul(out=warm_ps[:], lhsT=ones[:], rhs=zeros[:], start=True, stop=True)
+        raise_clock(4)
 
         nc.vector.tensor_copy(out=brow[0:1, :], in_=bland[0:1, :])
         bkq_ps = ps_kq.tile([P, 2 * E], F32, name="bkq_ps", tag="kq")
@@ -130,11 +129,12 @@ def tile_attention_t_kernel(tc, x, Wk, bk, Wq, bq, Wv, bv, out_0, out_1, out_2):
         wscl = const.tile([P, 2, 6 * P], U8, name="wscl", align_bytes=64)
         wgrp_w = wgrp[:].bitcast(F32).rearrange("p (g c r u) -> p g c r u", g=2, c=6, u=2)
 
-        def transposes(words, pool, tag):
+        def transposes(words, pool, tag, step=2):
             tb = pool.tile([P, 4, P], F32, name="tb_" + tag, tag=tag)
             for c in range(4):
                 g, u = divmod(c, 2)
-                nc.tensor.transpose(tb[:, c, :], words[:, 2 * P * g + u:2 * P * (g + 1):2], ident[:])
+                cols = slice(2 * P * g + u, 2 * P * (g + 1), 2) if step == 2 else slice(c * P, (c + 1) * P)
+                nc.tensor.transpose(tb[:, c, :], words[:, cols], ident[:])
             return tb[:].rearrange("p (g u) q -> p g q u", u=2)
 
         def weight_tile(col, raw, half, on_vector):
@@ -158,13 +158,27 @@ def tile_attention_t_kernel(tc, x, Wk, bk, Wq, bq, Wv, bv, out_0, out_1, out_2):
         banks = {}
         parts = {}
         cosines = {}
+        staged = {}
+
+        spread = {}
+
+        def split_words(i):
+            half = gpool.tile([P, D // 2], F32, name="half", tag="half", bufs=3)
+            nc.scalar.copy(
+                out=half[:].rearrange("p (g u m) -> p g u m", g=2, u=2),
+                in_=xs[i][:].bitcast(F32)[:, D // 2:D].rearrange("p (g m u) -> p g u m", g=2, u=2),
+            )
+            spread[i, 1] = half
 
         def front_a(i):
             grp = gpool.tile([P, 2 * D], BF16, name="grp", tag="grp", align_bytes=64)
             grp_w = grp[:].bitcast(F32).rearrange("p (s g q u) -> p s g q u", s=2, g=2, u=2)
             words = xs[i][:].bitcast(F32)
             for s in range(2):
-                src = transposes(words[:, s * (D // 2):(s + 1) * (D // 2)], ps_t, "t")
+                if (i, s) in spread:
+                    src = transposes(spread[i, s][:], ps_t, "t", 1)
+                else:
+                    src = transposes(words[:, s * (D // 2):(s + 1) * (D // 2)], ps_t, "t")
                 nc.scalar.copy(out=grp_w[:, s], in_=src)
             grouped[i] = grp
 
@@ -212,7 +226,7 @@ def tile_attention_t_kernel(tc, x, Wk, bk, Wq, bq, Wv, bv, out_0, out_1, out_2):
             return ap.rearrange("p (w j) -> p w j", w=2)
 
         def pool_adds_b1(i):
-            return 0 < i < PAIRS - 1
+            return 0 < i < PAIRS - 2
 
         def times_cos(i):
             kq = banks[i][0]
@@ -224,21 +238,33 @@ def tile_attention_t_kernel(tc, x, Wk, bk, Wq, bq, Wv, bv, out_0, out_1, out_2):
                 )
             cosines[i] = c_pair
 
-        def times_sin(i):
+        def times_sin(i, tiles=(0, 1)):
             kq = banks[i][0]
-            t_pair = tpool.tile([P, 2, 2 * E], F32, name="t_pair", tag="t_pair")
-            for s in range(2):
+            if i not in parts:
+                parts[i] = tpool.tile([P, 2, 2 * E], F32, name="t_pair", tag="t_pair")
+            for s in tiles:
                 nc.vector.scalar_tensor_tensor(
-                    out=t_pair[:, s, :], in0=kq[s][:], scalar=sin_t[:, s:s + 1], in1=bias_x[:, s, :],
+                    out=parts[i][:, s, :], in0=kq[s][:], scalar=sin_t[:, s:s + 1], in1=bias_x[:, s, :],
                     op0=ALU.mult, op1=ALU.add,
                 )
-            parts[i] = t_pair
 
-        def back_second(i):
-            kq, vb = banks[i]
+        def stage(i):
+            if i not in staged:
+                staged[i] = opool.tile([P, 3, 2, E], F32, name="stage", tag="stage")
+            return staged[i]
+
+        def v_out(i):
+            o = stage(i)
+            nc.vector.tensor_tensor(
+                out=o[:, 2, :, :], in0=banks[i][1][:], in1=b_v[:].unsqueeze(1).to_broadcast([P, 2, E]), op=ALU.add
+            )
+            nc.sync.dma_start(out=outs[2][i], in_=o[:, 2, :, :].rearrange("p s e -> p (s e)"))
+
+        def rope_adds(i):
+            kq = banks[i][0]
             t_pair = parts[i]
             c_pair = cosines[i]
-            o = opool.tile([P, 3, 2, E], F32, name="stage", tag="stage")
+            o = stage(i)
             nc.gpsimd.tensor_tensor(
                 out=o[:, 0:2, :, 0:P],
                 in0=c_pair[:, :, 0:E].rearrange("p s (w j) -> p w s j", w=2),
@@ -256,24 +282,44 @@ def tile_attention_t_kernel(tc, x, Wk, bk, Wq, bq, Wv, bv, out_0, out_1, out_2):
                         out=o[:, 0:2, s, P:2 * P], in0=halves(kq[s][:, E:2 * E]), scalar=cos_t[:, s:s + 1],
                         in1=halves(t_pair[:, s, 0:E]), op0=ALU.mult, op1=ALU.add,
                     )
-            nc.vector.tensor_tensor(
-                out=o[:, 2, :, :], in0=vb[:], in1=b_v[:].unsqueeze(1).to_broadcast([P, 2, E]), op=ALU.add
-            )
-            for n in (2, 0, 1):
-                nc.sync.dma_start(out=outs[n][i], in_=o[:, n, :, :].rearrange("p s e -> p (s e)"))
+
+        def rope_stores(i):
+            for n in (0, 1):
+                nc.sync.dma_start(out=outs[n][i], in_=staged[i][:, n, :, :].rearrange("p s e -> p (s e)"))
+
+        def last_pair(i):
+            kq = banks[i][0]
+            v_out(i)
+            o = staged[i]
+            for s in range(2):
+                times_sin(i, (s,))
+                nc.gpsimd.tensor_tensor(
+                    out=o[:, 0:2, s, 0:P], in0=halves(cosines[i][:, s, 0:E]), in1=halves(parts[i][:, s, E:2 * E]),
+                    op=ALU.subtract,
+                )
+                nc.vector.scalar_tensor_tensor(
+                    out=o[:, 0:2, s, P:2 * P], in0=halves(kq[s][:, E:2 * E]), scalar=cos_t[:, s:s + 1],
+                    in1=halves(parts[i][:, s, 0:E]), op0=ALU.mult, op1=ALU.add,
+                )
+                for n in (0, 1):
+                    nc.sync.dma_start(out=outs[n][i][:, s * E:(s + 1) * E], in_=o[:, n, s, :])
+
+        def back_second(i):
+            rope_adds(i)
+            rope_stores(i)
 
         weight_tile(0, wraw[0], 0, False)
         weight_tile(2, wraw[0], 1, True)
-        dummy(2)
+        raise_clock(2)
         weight_tile(1, wraw[1], 0, False)
         weight_tile(3, wraw[1], 1, True)
-        dummy(2)
+        raise_clock(2)
         weight_quant(0, 4)
         front_a(0)
         front_b(0)
         weight_tile(4, wraw[2], 0, False)
         weight_tile(5, wraw[2], 1, False)
-        dummy(2)
+        raise_clock(2)
         weight_quant(4, 6)
         front_a(1)
         front_b(1)
@@ -286,10 +332,21 @@ def tile_attention_t_kernel(tc, x, Wk, bk, Wq, bq, Wv, bv, out_0, out_1, out_2):
         for i in range(PAIRS):
             if i + 1 < PAIRS:
                 times_cos(i + 1)
-            times_sin(i)
-            if i + 2 < PAIRS:
-                front_b(i + 2)
-            back_second(i)
+            if i == PAIRS - 1:
+                last_pair(i)
+            elif i >= PAIRS - 1:
+                v_out(i)
+                times_sin(i)
+                back_second(i)
+            else:
+                times_sin(i)
+                if i + 2 < PAIRS:
+                    front_b(i + 2)
+                rope_adds(i)
+                v_out(i)
+                rope_stores(i)
+            if i % 2 == 1 and i + 4 < PAIRS:
+                split_words(i + 4)
             if i + 3 < PAIRS:
                 front_a(i + 3)
             if i + 2 < PAIRS:

@@ -310,16 +310,13 @@ def tile_attention_t_kernel(tc, x, Wk, bk, Wq, bq, Wv, bv, out_0, out_1, out_2):
 
         weight_tile(0, wraw[0], 0, False)
         weight_tile(2, wraw[0], 1, True)
-        raise_clock(2)
         weight_tile(1, wraw[1], 0, False)
         weight_tile(3, wraw[1], 1, True)
-        raise_clock(2)
         weight_quant(0, 4)
         front_a(0)
         front_b(0)
         weight_tile(4, wraw[2], 0, False)
         weight_tile(5, wraw[2], 1, False)
-        raise_clock(2)
         weight_quant(4, 6)
         front_a(1)
         front_b(1)

@@ -92,7 +92,7 @@ def tile_attention_t_kernel(tc, x, Wk, bk, Wq, bq, Wv, bv, out_0, out_1, out_2):
         nc.scalar.activation(out=s_half[:], in_=theta[:], func=ACT.Sin, scale=0.5)
         nc.scalar.activation(out=s_quart[:], in_=theta[:], func=ACT.Sin, scale=0.25)
 
-        raise_clock(4)
+        raise_clock(3)
 
         nc.vector.tensor_copy(out=brow[0:1, :], in_=bland[0:1, :])
         bkq_ps = ps_kq.tile([P, 2 * E], F32, name="bkq_ps", tag="kq")
@@ -228,15 +228,15 @@ def tile_attention_t_kernel(tc, x, Wk, bk, Wq, bq, Wv, bv, out_0, out_1, out_2):
         def pool_adds_b1(i):
             return 0 < i < PAIRS - 2
 
-        def times_cos(i):
+        def times_cos(i, tiles=(0, 1)):
             kq = banks[i][0]
-            c_pair = tpool.tile([P, 2, 2 * E], F32, name="c_pair", tag="c_pair")
-            for s in range(2):
+            if i not in cosines:
+                cosines[i] = tpool.tile([P, 2, 2 * E], F32, name="c_pair", tag="c_pair")
+            for s in tiles:
                 width = 2 * E if (s == 1 and pool_adds_b1(i)) else E
                 nc.scalar.activation(
-                    out=c_pair[:, s, 0:width], in_=kq[s][:, 0:width], func=ACT.Copy, scale=cos_t[:, s:s + 1]
+                    out=cosines[i][:, s, 0:width], in_=kq[s][:, 0:width], func=ACT.Copy, scale=cos_t[:, s:s + 1]
                 )
-            cosines[i] = c_pair
 
         def times_sin(i, tiles=(0, 1)):
             kq = banks[i][0]
@@ -323,10 +323,13 @@ def tile_attention_t_kernel(tc, x, Wk, bk, Wq, bq, Wv, bv, out_0, out_1, out_2):
         mx_pair(0)
         bias_table(0)
         bias_table(1)
-        times_cos(0)
+        times_cos(0, (0,))
         front_a(2)
         mx_pair(1)
         for i in range(PAIRS):
+            if i == 0:
+                times_sin(i)
+                times_cos(i, (1,))
             if i + 1 < PAIRS:
                 times_cos(i + 1)
             if i == PAIRS - 1:
@@ -336,7 +339,8 @@ def tile_attention_t_kernel(tc, x, Wk, bk, Wq, bq, Wv, bv, out_0, out_1, out_2):
                 times_sin(i)
                 back_second(i)
             else:
-                times_sin(i)
+                if i > 0:
+                    times_sin(i)
                 if i + 2 < PAIRS:
                     front_b(i + 2)
                 rope_adds(i)

import math
from contextlib import ExitStack

import concourse.mybir as mybir
from concourse.masks import make_identity

FLOPS = 2 * 4096 * 1024 * 768

F32 = mybir.dt.float32
BF16 = mybir.dt.bfloat16
I32 = mybir.dt.int32
U32 = mybir.dt.uint32
U8 = mybir.dt.uint8
FP8X4 = mybir.dt.float8_e4m3fn_x4
ALU = mybir.AluOpType
ACT = mybir.ActivationFunctionType

P = 128
D = 1024
E = 256
TOKENS = 4096
PAIRS = TOKENS // (2 * P)


def tile_attention_t_kernel(tc, x, Wk, bk, Wq, bq, Wv, bv, out_0, out_1, out_2):
    nc = tc.nc
    with ExitStack() as ctx:
        ctx.enter_context(tc.manual_schedule())
        const = ctx.enter_context(tc.tile_pool(name="const", bufs=1))
        xpool = ctx.enter_context(tc.tile_pool(name="xpool", bufs=1))
        gpool = ctx.enter_context(tc.tile_pool(name="gpool", bufs=2))
        cpool = ctx.enter_context(tc.tile_pool(name="cpool", bufs=4))
        tpool = ctx.enter_context(tc.tile_pool(name="tpool", bufs=4))
        opool = ctx.enter_context(tc.tile_pool(name="opool", bufs=8))
        ps_t = ctx.enter_context(tc.psum_pool(name="ps_t", bufs=2))
        ps_kq = ctx.enter_context(tc.psum_pool(name="ps_kq", bufs=4))
        ps_v = ctx.enter_context(tc.psum_pool(name="ps_v", bufs=2))

        xv = x.flatten_outer_dims().rearrange("(i q s) d -> i q (s d)", q=P, s=2)
        outs = [
            o.flatten_outer_dims().rearrange("(i q s) e -> i q (s e)", q=P, s=2)
            for o in (out_0, out_1, out_2)
        ]

        bland = const.tile([P, 3 * E], BF16, name="bland")
        for n, b in enumerate((bk, bq, bv)):
            nc.sync.dma_start(out=bland[0:1, n * E:(n + 1) * E], in_=b.rearrange("(o e) -> o e", o=1))
        wraw = []
        for n in range(3):
            wraw.append(const.tile([P, 2 * D], BF16, name="wraw%d" % n))
        xs = []
        for i in range(PAIRS):
            xs.append(xpool.tile([P, 2 * D], BF16, name="xs%d" % i))
        for h in range(2):
            nc.sync.dma_start(out=wraw[0][:, h * D:(h + 1) * D], in_=Wk.rearrange("(j h) d -> j (h d)", h=2)[:, h * D:(h + 1) * D])
        nc.sync.dma_start(out=wraw[1][:], in_=Wq.rearrange("(j h) d -> j (h d)", h=2))
        nc.sync.dma_start(out=xs[0][:], in_=xv[0])
        nc.sync.dma_start(
            out=wraw[2][:].rearrange("j (h d) -> j h d", h=2),
            in_=Wv.rearrange("(h j) d -> j h d", h=2),
        )
        for i in range(1, PAIRS):
            nc.sync.dma_start(out=xs[i][:], in_=xv[i])

        brow = const.tile([P, 3 * E], BF16, name="brow")
        ones = const.tile([P, P], BF16, name="ones")
        nc.vector.memset(brow[:], 0.0)
        nc.vector.memset(ones[:], 1.0)
        zeros = const.tile([P, 2 * E], BF16, name="zeros")
        nc.gpsimd.memset(zeros[:], 0.0)

        def raise_clock(n):
            for i in range(n):
                idle = ps_t.tile([P, 2 * E], F32, name="idle", tag="t")
                nc.tensor.matmul(out=idle[:], lhsT=ones[:], rhs=zeros[:], start=True, stop=True)

        pos_i = const.tile([P, 2], I32, name="pos_i")
        nc.gpsimd.iota(pos_i[:], pattern=[[1, 2]], base=0, channel_multiplier=2)
        ident = const.tile([P, P], F32, name="ident")
        make_identity(nc, ident[:])

        pos_m = const.tile([P, 2], I32, name="pos_m")
        nc.vector.tensor_single_scalar(out=pos_m[:], in_=pos_i[:], scalar=127, op=ALU.bitwise_and)
        pos_f = const.tile([P, 2], F32, name="pos_f")
        nc.vector.tensor_copy(out=pos_f[:], in_=pos_m[:])
        decay = const.tile([P, 2], F32, name="decay")
        nc.scalar.activation(out=decay[:], in_=pos_f[:], func=ACT.Exp, scale=-math.log(10000.0) / 128.0)
        theta = const.tile([P, 2], F32, name="theta")
        nc.vector.tensor_tensor(out=theta[:], in0=pos_f[:], in1=decay[:], op=ALU.mult)
        s_half = const.tile([P, 2], F32, name="s_half")
        s_quart = const.tile([P, 2], F32, name="s_quart")
        nc.scalar.activation(out=s_half[:], in_=theta[:], func=ACT.Sin, scale=0.5)
        nc.scalar.activation(out=s_quart[:], in_=theta[:], func=ACT.Sin, scale=0.25)

        raise_clock(3)

        nc.vector.tensor_copy(out=brow[0:1, :], in_=bland[0:1, :])
        bkq_ps = ps_kq.tile([P, 2 * E], F32, name="bkq_ps", tag="kq")
        bv_ps = ps_v.tile([P, 2, E], F32, name="bv_ps", tag="v")
        nc.tensor.matmul(out=bkq_ps[:], lhsT=ones[:], rhs=brow[:, 0:2 * E], start=True, stop=True)
        nc.tensor.matmul(out=bv_ps[:, 0, :], lhsT=ones[:], rhs=brow[:, 2 * E:3 * E], start=True, stop=True)
        b_eo = const.tile([P, 2 * E], F32, name="b_eo")
        b_sw = const.tile([P, 2 * E], F32, name="b_sw")
        b_v = const.tile([P, E], F32, name="b_v")
        bkq_view = bkq_ps[:].rearrange("p (w j h) -> p h w j", w=2, h=2)
        nc.scalar.copy(out=b_eo[:].rearrange("p (h w j) -> p h w j", h=2, w=2), in_=bkq_view)
        nc.vector.tensor_copy(out=b_sw[:, 0:E].rearrange("p (w j) -> p w j", w=2), in_=bkq_view[:, 1])
        nc.vector.tensor_scalar(
            out=b_sw[:, E:2 * E].rearrange("p (w j) -> p w j", w=2), in0=bkq_view[:, 0],
            scalar1=-1.0, scalar2=None, op0=ALU.mult,
        )
        nc.scalar.copy(out=b_v[:], in_=bv_ps[:, 0, :])

        sq_q = const.tile([P, 2], F32, name="sq_q")
        c_half = const.tile([P, 2], F32, name="c_half")
        sin_t = const.tile([P, 2], F32, name="sin_t")
        sq_h = const.tile([P, 2], F32, name="sq_h")
        cos_t = const.tile([P, 2], F32, name="cos_t")
        nc.vector.tensor_tensor(out=sq_q[:], in0=s_quart[:], in1=s_quart[:], op=ALU.mult)
        nc.vector.tensor_tensor(out=sq_h[:], in0=s_half[:], in1=s_half[:], op=ALU.mult)
        nc.vector.tensor_scalar(out=c_half[:], in0=sq_q[:], scalar1=-2.0, scalar2=1.0, op0=ALU.mult, op1=ALU.add)
        nc.vector.tensor_scalar(out=cos_t[:], in0=sq_h[:], scalar1=-2.0, scalar2=1.0, op0=ALU.mult, op1=ALU.add)
        nc.vector.scalar_tensor_tensor(
            out=sin_t[:], in0=s_half[:], scalar=2.0, in1=c_half[:], op0=ALU.mult, op1=ALU.mult
        )

        wgrp = const.tile([P, 2 * 6 * 4 * P], BF16, name="wgrp", align_bytes=64)
        wcod = const.tile([P, 2, 6 * P], U32, name="wcod", align_bytes=64)
        wscl = const.tile([P, 2, 6 * P], U8, name="wscl", align_bytes=64)
        wgrp_w = wgrp[:].bitcast(F32).rearrange("p (g c r u) -> p g c r u", g=2, c=6, u=2)

        def transposes(words, pool, tag, step=2):
            tb = pool.tile([P, 4, P], F32, name="tb_" + tag, tag=tag)
            for c in range(4):
                g, u = divmod(c, 2)
                cols = slice(2 * P * g + u, 2 * P * (g + 1), 2) if step == 2 else slice(c * P, (c + 1) * P)
                nc.tensor.transpose(tb[:, c, :], words[:, cols], ident[:])
            return tb[:].rearrange("p (g u) q -> p g q u", u=2)

        def weight_tile(col, raw, half, on_vector):
            pool, tag = (ps_kq, "kq") if col < 4 else (ps_v, "v")
            src = transposes(raw[:].bitcast(F32)[:, half * (D // 2):(half + 1) * (D // 2)], pool, tag)
            if on_vector:
                nc.vector.tensor_copy(out=wgrp_w[:, :, col], in_=src)
            else:
                nc.scalar.copy(out=wgrp_w[:, :, col], in_=src)

        def weight_quant(lo, hi):
            for g in range(2):
                nc.vector.quantize_mx(
                    out=wcod[:, g, lo * P:hi * P].bitcast(FP8X4),
                    scales=wscl[:, g, lo * P:hi * P],
                    in_=wgrp[:, (g * 6 + lo) * 4 * P:(g * 6 + hi) * 4 * P],
                )

        grouped = {}
        codes = {}
        banks = {}
        parts = {}
        cosines = {}
        staged = {}

        spread = {}

        def split_words(i):
            half = gpool.tile([P, D // 2], F32, name="half", tag="half", bufs=3)
            nc.scalar.copy(
                out=half[:].rearrange("p (g u m) -> p g u m", g=2, u=2),
                in_=xs[i][:].bitcast(F32)[:, D // 2:D].rearrange("p (g m u) -> p g u m", g=2, u=2),
            )
            spread[i, 1] = half

        def front_a(i):
            grp = gpool.tile([P, 2 * D], BF16, name="grp", tag="grp", align_bytes=64)
            grp_w = grp[:].bitcast(F32).rearrange("p (s g q u) -> p s g q u", s=2, g=2, u=2)
            words = xs[i][:].bitcast(F32)
            for s in range(2):
                if (i, s) in spread:
                    src = transposes(spread[i, s][:], ps_t, "t", 1)
                else:
                    src = transposes(words[:, s * (D // 2):(s + 1) * (D // 2)], ps_t, "t")
                nc.scalar.copy(out=grp_w[:, s], in_=src)
            grouped[i] = grp

        def front_b(i):
            cod = cpool.tile([P, 4 * P], U32, name="cod", tag="cod", align_bytes=64)
            scl = cpool.tile([P, 4 * P], U8, name="scl", tag="scl", align_bytes=64)
            nc.vector.quantize_mx(out=cod[:].bitcast(FP8X4), scales=scl[:], in_=grouped[i][:])
            codes[i] = (cod, scl)

        bias_x = const.tile([P, 2, 2 * E], F32, name="bias_x")

        def bias_table(s):
            tmp = tpool.tile([P, 2 * E], F32, name="tmp", tag="tmp", bufs=2)
            nc.scalar.activation(out=tmp[:], in_=b_sw[:], func=ACT.Copy, scale=cos_t[:, s:s + 1])
            nc.vector.scalar_tensor_tensor(
                out=bias_x[:, s, :], in0=b_eo[:], scalar=sin_t[:, s:s + 1], in1=tmp[:],
                op0=ALU.mult, op1=ALU.add,
            )

        def mx_pair(i):
            cod, scl = codes[i]
            kq = []
            for s in range(2):
                acc = ps_kq.tile([P, 2 * E], F32, name="kq", tag="kq")
                for g in range(2):
                    cols = slice((2 * s + g) * P, (2 * s + g + 1) * P)
                    nc.tensor.matmul_mx(
                        out=acc[:], lhsT=cod[:, cols].bitcast(FP8X4), lhsT_scale=scl[:, cols],
                        rhs=wcod[:, g, 0:4 * P].bitcast(FP8X4), rhs_scale=wscl[:, g, 0:4 * P],
                        start=(g == 0), stop=(g == 1),
                    )
                kq.append(acc)
            vb = ps_v.tile([P, 2, E], F32, name="vb", tag="v")
            for s in range(2):
                for g in range(2):
                    cols = slice((2 * s + g) * P, (2 * s + g + 1) * P)
                    nc.tensor.matmul_mx(
                        out=vb[:, s, :], lhsT=cod[:, cols].bitcast(FP8X4), lhsT_scale=scl[:, cols],
                        rhs=wcod[:, g, 4 * P:6 * P].bitcast(FP8X4), rhs_scale=wscl[:, g, 4 * P:6 * P],
                        start=(g == 0), stop=(g == 1),
                    )
            banks[i] = (kq, vb)

        def halves(ap):
            return ap.rearrange("p (w j) -> p w j", w=2)

        def pool_adds_b1(i):
            return 0 < i < PAIRS - 2

        def times_cos(i, tiles=(0, 1)):
            kq = banks[i][0]
            if i not in cosines:
                cosines[i] = tpool.tile([P, 2, 2 * E], F32, name="c_pair", tag="c_pair")
            for s in tiles:
                width = 2 * E if (s == 1 and pool_adds_b1(i)) else E
                nc.scalar.activation(
                    out=cosines[i][:, s, 0:width], in_=kq[s][:, 0:width], func=ACT.Copy, scale=cos_t[:, s:s + 1]
                )

        def times_sin(i, tiles=(0, 1)):
            kq = banks[i][0]
            if i not in parts:
                parts[i] = tpool.tile([P, 2, 2 * E], F32, name="t_pair", tag="t_pair")
            for s in tiles:
                nc.vector.scalar_tensor_tensor(
                    out=parts[i][:, s, :], in0=kq[s][:], scalar=sin_t[:, s:s + 1], in1=bias_x[:, s, :],
                    op0=ALU.mult, op1=ALU.add,
                )

        def stage(i):
            if i not in staged:
                staged[i] = opool.tile([P, 3, 2, E], F32, name="stage", tag="stage")
            return staged[i]

        def v_out(i):
            o = stage(i)
            nc.vector.tensor_tensor(
                out=o[:, 2, :, :], in0=banks[i][1][:], in1=b_v[:].unsqueeze(1).to_broadcast([P, 2, E]), op=ALU.add
            )
            nc.sync.dma_start(out=outs[2][i], in_=o[:, 2, :, :].rearrange("p s e -> p (s e)"))

        def rope_adds(i):
            kq = banks[i][0]
            t_pair = parts[i]
            c_pair = cosines[i]
            o = stage(i)
            nc.gpsimd.tensor_tensor(
                out=o[:, 0:2, :, 0:P],
                in0=c_pair[:, :, 0:E].rearrange("p s (w j) -> p w s j", w=2),
                in1=t_pair[:, :, E:2 * E].rearrange("p s (w j) -> p w s j", w=2),
                op=ALU.subtract,
            )
            for s in range(2):
                if s == 1 and pool_adds_b1(i):
                    nc.gpsimd.tensor_tensor(
                        out=o[:, 0:2, s, P:2 * P], in0=halves(c_pair[:, s, E:2 * E]),
                        in1=halves(t_pair[:, s, 0:E]), op=ALU.add,
                    )
                else:
                    nc.vector.scalar_tensor_tensor(
                        out=o[:, 0:2, s, P:2 * P], in0=halves(kq[s][:, E:2 * E]), scalar=cos_t[:, s:s + 1],
                        in1=halves(t_pair[:, s, 0:E]), op0=ALU.mult, op1=ALU.add,
                    )

        def rope_stores(i):
            for n in (0, 1):
                nc.sync.dma_start(out=outs[n][i], in_=staged[i][:, n, :, :].rearrange("p s e -> p (s e)"))

        def last_pair(i):
            kq = banks[i][0]
            v_out(i)
            o = staged[i]
            for s in range(2):
                times_sin(i, (s,))
                nc.gpsimd.tensor_tensor(
                    out=o[:, 0:2, s, 0:P], in0=halves(cosines[i][:, s, 0:E]), in1=halves(parts[i][:, s, E:2 * E]),
                    op=ALU.subtract,
                )
                nc.vector.scalar_tensor_tensor(
                    out=o[:, 0:2, s, P:2 * P], in0=halves(kq[s][:, E:2 * E]), scalar=cos_t[:, s:s + 1],
                    in1=halves(parts[i][:, s, 0:E]), op0=ALU.mult, op1=ALU.add,
                )
                for n in (0, 1):
                    nc.sync.dma_start(out=outs[n][i][:, s * E:(s + 1) * E], in_=o[:, n, s, :])

        def back_second(i):
            rope_adds(i)
            rope_stores(i)

        weight_tile(0, wraw[0], 0, False)
        weight_tile(2, wraw[0], 1, True)
        weight_tile(1, wraw[1], 0, False)
        weight_tile(3, wraw[1], 1, True)
        weight_quant(0, 4)
        front_a(0)
        front_b(0)
        weight_tile(4, wraw[2], 0, False)
        weight_tile(5, wraw[2], 1, False)
        weight_quant(4, 6)
        front_a(1)
        front_b(1)
        mx_pair(0)
        bias_table(0)
        bias_table(1)
        times_cos(0, (0,))
        front_a(2)
        mx_pair(1)
        for i in range(PAIRS):
            if i == 0:
                times_sin(i)
                times_cos(i, (1,))
            if i + 1 < PAIRS:
                times_cos(i + 1)
            if i == PAIRS - 1:
                last_pair(i)
            elif i >= PAIRS - 1:
                v_out(i)
                times_sin(i)
                back_second(i)
            else:
                if i > 0:
                    times_sin(i)
                if i + 2 < PAIRS:
                    front_b(i + 2)
                rope_adds(i)
                v_out(i)
                rope_stores(i)
            if i % 2 == 1 and i + 4 < PAIRS:
                split_words(i + 4)
            if i + 3 < PAIRS:
                front_a(i + 3)
            if i + 2 < PAIRS:
                mx_pair(i + 2)
